import numpy as np
import ml_dtypes


def mxq(x, axis, fmt="e4m3"):
    dtype, down = {"e4m3": (ml_dtypes.float8_e4m3fn, 7), "e5m2": (ml_dtypes.float8_e5m2, 14)}[fmt]
    v = np.moveaxis(np.asarray(x, np.float32).astype(ml_dtypes.bfloat16).astype(np.float64), axis, -1)
    blocks = v.reshape(v.shape[:-1] + (-1, 32))
    amax = np.abs(blocks).max(-1, keepdims=True)
    byte = np.maximum(np.where(amax > 0, np.frexp(amax)[1] - 1 + 127, 0) - down, 1)
    scale = np.exp2(byte - 127.0)
    codes = (blocks / scale).astype(np.float32).astype(dtype).astype(np.float64)
    return np.moveaxis((codes * scale).reshape(v.shape), -1, axis)


WIDE = False


def mx_kscale(k):
    if not WIDE:
        return np.ones(k)
    levels = np.array([10, -10, 5, -5, 0])
    a = np.random.permutation(np.resize(levels, k // 512 * 4)).reshape(k // 512, 4)
    idx = np.arange(k)
    return np.exp2(a[idx // 512, idx % 128 // 32])


BF16 = ml_dtypes.bfloat16


def bf(x):
    return np.asarray(x, np.float32).astype(BF16)


def f64(x):
    return np.asarray(x).astype(np.float64)


E2M1 = np.array([0.0, 0.5, 1.0, 1.5, 2.0, 3.0, 4.0, 6.0, -0.0, -0.5, -1.0, -1.5, -2.0, -3.0, -4.0, -6.0])


def pack_weight(w, fmt):
    k, n = w.shape
    w = f64(bf(w)).reshape(k // 32, 32, n)
    amax = np.abs(w).max(1)
    if fmt == "e4m3":
        byte = np.frexp(amax)[1] - 1 + 127 - 7
    else:
        mant, ex = np.frexp(amax / 6.0)
        byte = np.where(mant > 0.5, ex, ex - 1) + 127
    byte = np.clip(np.where(amax > 0, byte, 1), 1, 254)
    scaled = (w * np.exp2(127.0 - byte)[:, None, :]).reshape(k, n).astype(np.float32)
    by_word = np.ascontiguousarray(scaled.reshape(k // 512, 128, 4, n).transpose(0, 1, 3, 2))
    if fmt == "e4m3":
        words = by_word.astype(ml_dtypes.float8_e4m3fn).view(np.uint8)
    else:
        c = by_word.astype(ml_dtypes.float4_e2m1fn).view(np.uint8) & 0xF
        words = c[..., 0::2] | (c[..., 1::2] << 4)
    return np.ascontiguousarray(words), np.ascontiguousarray(byte.astype(np.uint8).reshape(k // 512, 16, n))


def unpack_weight(words, scales, fmt):
    g, p, n, _ = words.shape
    if fmt == "e4m3":
        vals = np.ascontiguousarray(words).view(ml_dtypes.float8_e4m3fn).astype(np.float64)
    else:
        nib = np.empty((g, p, n, 4), np.uint8)
        nib[..., 0::2] = words & 0xF
        nib[..., 1::2] = words >> 4
        vals = E2M1[nib]
    vals = vals * np.repeat(np.exp2(scales.astype(np.float64) - 127.0), 8, axis=1)[..., None]
    return vals.transpose(0, 1, 3, 2).reshape(g * 512, n)

def pack4(w):
    words, scales = pack_weight(w, "e2m1")
    return words.reshape(words.shape[0], 128, -1), scales


def unpack4(words, scales):
    return unpack_weight(words.reshape(words.shape[0], 128, -1, 2), scales, "e2m1")


B, C, HH, WW, NH, HD, F = 32, 256, 16, 16, 8, 64, 1024
EPS = 1e-5


def layer_norm(v, w, b):
    mu = v.mean(-1, keepdims=True)
    var = ((v - mu) ** 2).mean(-1, keepdims=True)
    return (v - mu) * (1.0 / np.sqrt(var + EPS)) * w + b


def setup_inputs():
    s = mx_kscale(F)
    h = bf(np.maximum(np.random.standard_normal((B, HH, WW, F)), 0.0) * 0.125 * s)
    ffn2_w = np.random.standard_normal((C, F)) * 0.5 / np.sqrt(F) / s
    words, scales = pack4(np.ascontiguousarray(ffn2_w.T))
    return {"h": h,
            "ffn2_w_words": words,
            "ffn2_w_scales": scales,
            "ffn2_b": bf(np.random.standard_normal(C) * 0.02),
            "scale_ffn": bf(0.1 * (1.0 + 0.1 * np.random.standard_normal(1))),
            "ln2_w": bf(1.0 + 0.1 * np.random.standard_normal(C)),
            "ln2_b": bf(0.1 * np.random.standard_normal(C)),
            "scale_norm2": bf(1.5 * (1.0 + 0.1 * np.random.standard_normal(1))),
            "x": bf(np.random.standard_normal((B, C, HH, WW)))}


def reference(h, ffn2_w_words, ffn2_w_scales, ffn2_b, scale_ffn, ln2_w, ln2_b, scale_norm2, x):
    y2 = ((mxq(f64(h), 3, "e4m3") @ unpack4(ffn2_w_words, ffn2_w_scales)) + f64(ffn2_b)) * f64(scale_ffn)
    y2 = layer_norm(y2, f64(ln2_w), f64(ln2_b)) * f64(scale_norm2)
    out = np.maximum(y2 + f64(x).transpose(0, 2, 3, 1), 0.0)
    return out.transpose(0, 3, 1, 2)

@@ -1,0 +1,271 @@
+from contextlib import ExitStack
+
+import concourse.mybir as mybir
+from concourse.masks import make_identity
+
+F32 = mybir.dt.float32
+BF16 = mybir.dt.bfloat16
+I32 = mybir.dt.int32
+U32 = mybir.dt.uint32
+U8 = mybir.dt.uint8
+FP8X4 = mybir.dt.float8_e4m3fn_x4
+FP4X4 = mybir.dt.float4_e2m1fn_x4
+ACT = mybir.ActivationFunctionType
+ALU = mybir.AluOpType
+
+P = 128
+PACK = 4
+IMAGES = 32
+PIXELS = 256
+TILES = PIXELS // P
+K = 1024
+PASSES = K // (P * PACK)
+CH = 256
+PAIR = CH // P
+EPS = 1e-5
+X_GROUP = 4
+H_AHEAD = 3
+F32_MAX = 3.4028234663852886e38
+
+FLOPS = 2 * IMAGES * PIXELS * K * CH
+
+
+def tile_transformerconvblock_pc_t_kernel(
+    tc, h, ffn2_w_words, ffn2_w_scales, ffn2_b, scale_ffn, ln2_w, ln2_b, scale_norm2, x, out
+):
+    nc = tc.nc
+    h_rows = h.flatten_outer_dims()
+
+    with ExitStack() as stack:
+        const = stack.enter_context(tc.tile_pool(name="const", bufs=1))
+        h_pool = stack.enter_context(tc.tile_pool(name="h_pool", bufs=H_AHEAD + 2))
+        mx_pool = stack.enter_context(tc.tile_pool(name="mx_pool", bufs=3))
+        norm_pool = stack.enter_context(tc.tile_pool(name="norm_pool", bufs=3))
+        stat_pool = stack.enter_context(tc.tile_pool(name="stat_pool", bufs=4))
+        x_pool = stack.enter_context(tc.tile_pool(name="x_pool", bufs=2))
+        y_pool = stack.enter_context(tc.tile_pool(name="y_pool", bufs=3))
+        psum_h = stack.enter_context(tc.psum_pool(name="psum_h", bufs=2 * TILES))
+        psum_acc = stack.enter_context(tc.psum_pool(name="psum_acc", bufs=2))
+        psum_out = stack.enter_context(tc.psum_pool(name="psum_out", bufs=2))
+        stack.enter_context(tc.manual_schedule())
+
+        h_tiles, grouped_tiles, code_tiles, plane_tiles = {}, {}, {}, {}
+        acc_tiles, u_tiles, sum_tiles, mean_tiles, std_tiles = {}, {}, {}, {}, {}
+        v_tiles, back_tiles, x_tiles, shortcut_tiles = {}, {}, {}, {}
+
+        def load_h(i):
+            h_sb = h_pool.tile([P, TILES, K], BF16)
+            nc.sync.dma_start(
+                out=h_sb[:],
+                in_=h_rows[i * PIXELS : (i + 1) * PIXELS, :].rearrange("(p t) k -> p t k", t=TILES),
+            )
+            h_tiles[i] = h_sb
+
+        load_h(0)
+        w_words = const.tile([P, PASSES, 2 * CH], U8, align_bytes=64)
+        nc.sync.dma_start(
+            out=w_words[:].bitcast(I32), in_=ffn2_w_words.bitcast(I32).rearrange("g p n -> p g n")
+        )
+        w_planes = const.tile([P, PASSES, CH], U8, align_bytes=64)
+        nc.vector.memset(w_planes[:].bitcast(I32), 0)
+        for quad in range(4):
+            nc.sync.dma_start(
+                out=w_planes[32 * quad : 32 * quad + 4].bitcast(I32),
+                in_=ffn2_w_scales[:, 4 * quad : 4 * quad + 4, :].bitcast(I32).rearrange("g r n -> r g n"),
+            )
+        for i in range(1, H_AHEAD):
+            load_h(i)
+
+        bias_bf = const.tile([P, CH], BF16)
+        nc.scalar.dma_start(out=bias_bf[:], in_=ffn2_b.partition_broadcast(P))
+        scale_ffn_bf = const.tile([P, 1], BF16)
+        nc.scalar.dma_start(out=scale_ffn_bf[:], in_=scale_ffn.partition_broadcast(P))
+        scale_norm_bf = const.tile([P, 1], BF16)
+        nc.scalar.dma_start(out=scale_norm_bf[:], in_=scale_norm2.partition_broadcast(P))
+        ln_w_bf = const.tile([P, PAIR], BF16)
+        nc.scalar.dma_start(out=ln_w_bf[:], in_=ln2_w.rearrange("(c j) -> c j", j=PAIR))
+        ln_b_bf = const.tile([P, PAIR], BF16)
+        nc.scalar.dma_start(out=ln_b_bf[:], in_=ln2_b.rearrange("(c j) -> c j", j=PAIR))
+
+        ident = const.tile([P, P], F32)
+        make_identity(nc, ident[:])
+        scale_ffn_col = const.tile([P, 1], F32)
+        nc.vector.tensor_copy(out=scale_ffn_col[:], in_=scale_ffn_bf[:])
+        bias_scaled = const.tile([P, PAIR, P], F32)
+        nc.vector.tensor_scalar(
+            out=bias_scaled[:],
+            in0=bias_bf[:].rearrange("p (c j) -> p j c", j=PAIR),
+            scalar1=scale_ffn_col[:, 0:1],
+            scalar2=None,
+            op0=ALU.mult,
+        )
+        scale_norm_col = const.tile([P, 1], F32)
+        nc.vector.tensor_copy(out=scale_norm_col[:], in_=scale_norm_bf[:])
+        gain = const.tile([P, PAIR], F32)
+        nc.vector.tensor_scalar(
+            out=gain[:], in0=ln_w_bf[:], scalar1=scale_norm_col[:, 0:1], scalar2=None, op0=ALU.mult
+        )
+        shift = const.tile([P, PAIR], F32)
+        nc.vector.tensor_scalar(
+            out=shift[:], in0=ln_b_bf[:], scalar1=scale_norm_col[:, 0:1], scalar2=None, op0=ALU.mult
+        )
+
+        def load_x(q):
+            x_sb = x_pool.tile([P, X_GROUP, PAIR, PIXELS], BF16)
+            nc.sync.dma_start(
+                out=x_sb[:].rearrange("c b j x -> c b (j x)"),
+                in_=x[q * X_GROUP : (q + 1) * X_GROUP].rearrange("b (c j) y x -> c b (j y x)", j=PAIR),
+            )
+            x_tiles[q] = x_sb
+
+        def shift_x(q):
+            shortcut = x_pool.tile([P, X_GROUP, PAIR, PIXELS], F32)
+            for j in range(PAIR):
+                nc.gpsimd.tensor_scalar(
+                    out=shortcut[:, :, j, :],
+                    in0=x_tiles[q][:, :, j, :],
+                    scalar1=1.0,
+                    scalar2=shift[:, j : j + 1],
+                    op0=ALU.mult,
+                    op1=ALU.add,
+                )
+            shortcut_tiles[q] = shortcut
+
+        def transpose_h(i):
+            grouped = mx_pool.tile([P, TILES * PASSES * P * PACK], BF16, align_bytes=64)
+            grouped_words = grouped[:].bitcast(F32).rearrange(
+                "p (t g x w) -> p t g x w", t=TILES, g=PASSES, w=2
+            )
+            for t in range(TILES):
+                h_words = h_tiles[i][:, t, :].bitcast(F32)
+                h_t = psum_h.tile([P, PASSES, 2, P], F32)
+                for g in range(PASSES):
+                    for w in range(2):
+                        first = g * (K // PASSES // 2) + w
+                        nc.tensor.transpose(
+                            h_t[:, g, w, :], h_words[:, first : (g + 1) * (K // PASSES // 2) : 2], ident[:]
+                        )
+                nc.scalar.copy(out=grouped_words[:, t], in_=h_t[:].rearrange("p g w x -> p g x w"))
+            grouped_tiles[i] = grouped
+
+        def quantise(i):
+            codes = mx_pool.tile([P, TILES * PASSES * P], U32, align_bytes=64)
+            planes = mx_pool.tile([P, TILES * PASSES * P], U8, align_bytes=64)
+            nc.vector.quantize_mx(out=codes[:].bitcast(FP8X4), scales=planes[:], in_=grouped_tiles[i][:])
+            code_tiles[i], plane_tiles[i] = codes, planes
+
+        def multiply(i):
+            acc = psum_acc.tile([P, TILES, CH], F32)
+            for t in range(TILES):
+                for n in range(CH // P):
+                    for g in range(PASSES):
+                        pixels = slice((t * PASSES + g) * P, (t * PASSES + g + 1) * P)
+                        nc.tensor.matmul_mx(
+                            out=acc[:, t, n * P : (n + 1) * P],
+                            lhsT=code_tiles[i][:, pixels].bitcast(FP8X4),
+                            lhsT_scale=plane_tiles[i][:, pixels],
+                            rhs=w_words[:, g, 2 * n * P : 2 * (n + 1) * P].bitcast(FP4X4),
+                            rhs_scale=w_planes[:, g, n * P : (n + 1) * P],
+                            start=(g == 0),
+                            stop=(g == PASSES - 1),
+                        )
+            acc_tiles[i] = acc
+
+        def add_bias(i):
+            u = norm_pool.tile([P, TILES, PAIR, P], F32)
+            u_sum = stat_pool.tile([P, TILES], F32)
+            for t in range(TILES):
+                nc.vector.scalar_tensor_tensor(
+                    out=u[:, t],
+                    in0=acc_tiles[i][:, t, :].rearrange("p (c j) -> p j c", j=PAIR),
+                    scalar=scale_ffn_col[:, 0:1],
+                    in1=bias_scaled[:],
+                    op0=ALU.mult,
+                    op1=ALU.add,
+                    accum_out=u_sum[:, t : t + 1],
+                )
+            u_tiles[i], sum_tiles[i] = u, u_sum
+
+        def statistics(i):
+            neg_mean = stat_pool.tile([P, TILES], F32)
+            nc.scalar.mul(out=neg_mean[:], in_=sum_tiles[i][:], mul=-1.0 / CH)
+            dev_sq_sum = stat_pool.tile([P, TILES], F32)
+            for t in range(TILES):
+                squares = norm_pool.tile([P, CH], F32)
+                nc.scalar.activation(
+                    out=squares[:],
+                    in_=u_tiles[i][:, t].rearrange("p j c -> p (j c)"),
+                    func=ACT.Square,
+                    bias=neg_mean[:, t : t + 1],
+                    scale=1.0,
+                    accum_out=dev_sq_sum[:, t : t + 1],
+                )
+            std = stat_pool.tile([P, TILES], F32)
+            nc.scalar.activation(out=std[:], in_=dev_sq_sum[:], func=ACT.Sqrt, bias=EPS, scale=1.0 / CH)
+            mean_tiles[i], std_tiles[i] = neg_mean, std
+
+        def normalise(i):
+            rstd = stat_pool.tile([P, TILES], F32)
+            nc.vector.reciprocal(out=rstd[:], in_=std_tiles[i][:])
+            v = norm_pool.tile([P, TILES, PAIR, P], F32)
+            for t in range(TILES):
+                nc.vector.tensor_scalar(
+                    out=v[:, t],
+                    in0=u_tiles[i][:, t],
+                    scalar1=mean_tiles[i][:, t : t + 1],
+                    scalar2=rstd[:, t : t + 1],
+                    op0=ALU.add,
+                    op1=ALU.mult,
+                )
+            v_tiles[i] = v
+
+        def transpose_back(i):
+            back = psum_out.tile([P, PAIR, TILES, P], F32)
+            for j in range(PAIR):
+                for t in range(TILES):
+                    nc.tensor.transpose(back[:, j, t, :], v_tiles[i][:, t, j, :], ident[:])
+            back_tiles[i] = back
+
+        def finish(i):
+            y = y_pool.tile([P, PAIR, PIXELS], F32)
+            for j in range(PAIR):
+                nc.vector.scalar_tensor_tensor(
+                    out=y[:, j, :].rearrange("c (p t) -> c p t", t=TILES),
+                    in0=back_tiles[i][:, j].rearrange("c t p -> c p t"),
+                    scalar=gain[:, j : j + 1],
+                    in1=shortcut_tiles[i // X_GROUP][:, i % X_GROUP, j, :].rearrange("c (p t) -> c p t", t=TILES),
+                    op0=ALU.mult,
+                    op1=ALU.add,
+                )
+            nc.gpsimd.tensor_scalar(
+                out=y[:], in0=y[:], scalar1=F32_MAX, scalar2=0.0, op0=ALU.min, op1=ALU.max
+            )
+            nc.sync.dma_start(
+                out=out[i].rearrange("(c j) y x -> c (j y x)", j=PAIR), in_=y[:].rearrange("c j x -> c (j x)")
+            )
+
+        def live(i):
+            return 0 <= i < IMAGES
+
+        for s in range(IMAGES + 4):
+            if live(s + H_AHEAD):
+                load_h(s + H_AHEAD)
+            if s % X_GROUP == 0 and live(s):
+                load_x(s // X_GROUP)
+            if live(s - 3):
+                statistics(s - 3)
+            if live(s - 4):
+                transpose_back(s - 4)
+            if live(s):
+                transpose_h(s)
+            if live(s - 1):
+                quantise(s - 1)
+                multiply(s - 1)
+            if live(s - 2):
+                add_bias(s - 2)
+            if live(s - 4):
+                finish(s - 4)
+            if s % X_GROUP == 2 and live(s):
+                shift_x(s // X_GROUP)
+            if live(s - 3):
+                normalise(s - 3)

@@ -25,7 +25,6 @@ PAIR = CH // P
 EPS = 1e-5
 X_GROUP = 4
 H_AHEAD = 3
-F32_MAX = 3.4028234663852886e38
 
 FLOPS = 2 * IMAGES * PIXELS * K * CH
 
@@ -47,11 +46,10 @@ def tile_transformerconvblock_pc_t_kernel(
         psum_h = stack.enter_context(tc.psum_pool(name="psum_h", bufs=2 * TILES))
         psum_acc = stack.enter_context(tc.psum_pool(name="psum_acc", bufs=2))
         psum_out = stack.enter_context(tc.psum_pool(name="psum_out", bufs=2))
-        stack.enter_context(tc.manual_schedule())
 
         h_tiles, grouped_tiles, code_tiles, plane_tiles = {}, {}, {}, {}
-        acc_tiles, u_tiles, sum_tiles, mean_tiles, std_tiles = {}, {}, {}, {}, {}
-        v_tiles, back_tiles, x_tiles, shortcut_tiles = {}, {}, {}, {}
+        acc_tiles, u_tiles, sum_tiles, mean_tiles, rstd_tiles = {}, {}, {}, {}, {}
+        v_tiles, back_tiles, x_tiles = {}, {}, {}
 
         def load_h(i):
             h_sb = h_pool.tile([P, TILES, K], BF16)
@@ -117,19 +115,6 @@ def tile_transformerconvblock_pc_t_kernel(
                 in_=x[q * X_GROUP : (q + 1) * X_GROUP].rearrange("b (c j) y x -> c b (j y x)", j=PAIR),
             )
             x_tiles[q] = x_sb
-
-        def shift_x(q):
-            shortcut = x_pool.tile([P, X_GROUP, PAIR, PIXELS], F32)
-            for j in range(PAIR):
-                nc.gpsimd.tensor_scalar(
-                    out=shortcut[:, :, j, :],
-                    in0=x_tiles[q][:, :, j, :],
-                    scalar1=1.0,
-                    scalar2=shift[:, j : j + 1],
-                    op0=ALU.mult,
-                    op1=ALU.add,
-                )
-            shortcut_tiles[q] = shortcut
 
         def transpose_h(i):
             grouped = mx_pool.tile([P, TILES * PASSES * P * PACK], BF16, align_bytes=64)
@@ -200,24 +185,34 @@ def tile_transformerconvblock_pc_t_kernel(
                     scale=1.0,
                     accum_out=dev_sq_sum[:, t : t + 1],
                 )
-            std = stat_pool.tile([P, TILES], F32)
-            nc.scalar.activation(out=std[:], in_=dev_sq_sum[:], func=ACT.Sqrt, bias=EPS, scale=1.0 / CH)
-            mean_tiles[i], std_tiles[i] = neg_mean, std
-
-        def normalise(i):
             rstd = stat_pool.tile([P, TILES], F32)
-            nc.vector.reciprocal(out=rstd[:], in_=std_tiles[i][:])
-            v = norm_pool.tile([P, TILES, PAIR, P], F32)
-            for t in range(TILES):
-                nc.vector.tensor_scalar(
-                    out=v[:, t],
-                    in0=u_tiles[i][:, t],
-                    scalar1=mean_tiles[i][:, t : t + 1],
-                    scalar2=rstd[:, t : t + 1],
-                    op0=ALU.add,
-                    op1=ALU.mult,
-                )
-            v_tiles[i] = v
+            nc.scalar.activation(
+                out=rstd[:], in_=dev_sq_sum[:], func=ACT.Abs_reciprocal_sqrt, bias=EPS, scale=1.0 / CH
+            )
+            mean_tiles[i], rstd_tiles[i] = neg_mean, rstd
+
+        def normalise_on_scalar(i, v):
+            neg_mean_rstd = stat_pool.tile([P, 1], F32)
+            nc.scalar.activation(
+                out=neg_mean_rstd[:], in_=mean_tiles[i][:, 1:2], func=ACT.Copy, scale=rstd_tiles[i][:, 1:2]
+            )
+            nc.scalar.activation(
+                out=v[:, 1].rearrange("p j c -> p (j c)"),
+                in_=u_tiles[i][:, 1].rearrange("p j c -> p (j c)"),
+                func=ACT.Identity,
+                bias=neg_mean_rstd[:, 0:1],
+                scale=rstd_tiles[i][:, 1:2],
+            )
+
+        def normalise_on_vector(i, v):
+            nc.vector.tensor_scalar(
+                out=v[:, 0],
+                in0=u_tiles[i][:, 0],
+                scalar1=mean_tiles[i][:, 0:1],
+                scalar2=rstd_tiles[i][:, 0:1],
+                op0=ALU.add,
+                op1=ALU.mult,
+            )
 
         def transpose_back(i):
             back = psum_out.tile([P, PAIR, TILES, P], F32)
@@ -233,13 +228,14 @@ def tile_transformerconvblock_pc_t_kernel(
                     out=y[:, j, :].rearrange("c (p t) -> c p t", t=TILES),
                     in0=back_tiles[i][:, j].rearrange("c t p -> c p t"),
                     scalar=gain[:, j : j + 1],
-                    in1=shortcut_tiles[i // X_GROUP][:, i % X_GROUP, j, :].rearrange("c (p t) -> c p t", t=TILES),
+                    in1=x_tiles[i // X_GROUP][:, i % X_GROUP, j, :].rearrange("c (p t) -> c p t", t=TILES),
                     op0=ALU.mult,
                     op1=ALU.add,
                 )
-            nc.gpsimd.tensor_scalar(
-                out=y[:], in0=y[:], scalar1=F32_MAX, scalar2=0.0, op0=ALU.min, op1=ALU.max
-            )
+            for j in range(PAIR):
+                nc.vector.tensor_scalar(
+                    out=y[:, j, :], in0=y[:, j, :], scalar1=shift[:, j : j + 1], scalar2=0.0, op0=ALU.add, op1=ALU.max
+                )
             nc.sync.dma_start(
                 out=out[i].rearrange("(c j) y x -> c (j y x)", j=PAIR), in_=y[:].rearrange("c j x -> c (j x)")
             )
@@ -254,6 +250,9 @@ def tile_transformerconvblock_pc_t_kernel(
                 load_x(s // X_GROUP)
             if live(s - 3):
                 statistics(s - 3)
+                v = norm_pool.tile([P, TILES, PAIR, P], F32)
+                v_tiles[s - 3] = v
+                normalise_on_scalar(s - 3, v)
             if live(s - 4):
                 transpose_back(s - 4)
             if live(s):
@@ -263,9 +262,7 @@ def tile_transformerconvblock_pc_t_kernel(
                 multiply(s - 1)
             if live(s - 2):
                 add_bias(s - 2)
+            if live(s - 3):
+                normalise_on_vector(s - 3, v_tiles[s - 3])
             if live(s - 4):
                 finish(s - 4)
-            if s % X_GROUP == 2 and live(s):
-                shift_x(s // X_GROUP)
-            if live(s - 3):
-                normalise(s - 3)

@@ -25,6 +25,17 @@ PAIR = CH // P
 EPS = 1e-5
 X_GROUP = 4
 H_AHEAD = 3
+X_AHEAD = 4
+
+AT_COPY = 1
+AT_QUANTISE = 2
+AT_MULTIPLY = 3
+AT_BIAS = 4
+AT_STATISTICS = 5
+AT_NORMALISE = 6
+AT_BACK = 7
+AT_SHORTCUT = 8
+AT_RELU = 9
 
 FLOPS = 2 * IMAGES * PIXELS * K * CH
 
@@ -39,17 +50,18 @@ def tile_transformerconvblock_pc_t_kernel(
         const = stack.enter_context(tc.tile_pool(name="const", bufs=1))
         h_pool = stack.enter_context(tc.tile_pool(name="h_pool", bufs=H_AHEAD + 2))
         mx_pool = stack.enter_context(tc.tile_pool(name="mx_pool", bufs=3))
-        norm_pool = stack.enter_context(tc.tile_pool(name="norm_pool", bufs=3))
+        norm_pool = stack.enter_context(tc.tile_pool(name="norm_pool", bufs=4))
         stat_pool = stack.enter_context(tc.tile_pool(name="stat_pool", bufs=4))
         x_pool = stack.enter_context(tc.tile_pool(name="x_pool", bufs=2))
-        y_pool = stack.enter_context(tc.tile_pool(name="y_pool", bufs=3))
+        y_pool = stack.enter_context(tc.tile_pool(name="y_pool", bufs=4))
         psum_h = stack.enter_context(tc.psum_pool(name="psum_h", bufs=2 * TILES))
         psum_acc = stack.enter_context(tc.psum_pool(name="psum_acc", bufs=2))
-        psum_out = stack.enter_context(tc.psum_pool(name="psum_out", bufs=2))
+        psum_back = stack.enter_context(tc.psum_pool(name="psum_back", bufs=2))
+        stack.enter_context(tc.manual_schedule())
 
-        h_tiles, grouped_tiles, code_tiles, plane_tiles = {}, {}, {}, {}
-        acc_tiles, u_tiles, sum_tiles, mean_tiles, rstd_tiles = {}, {}, {}, {}, {}
-        v_tiles, back_tiles, x_tiles = {}, {}, {}
+        h_tiles, h_t_tiles, grouped_tiles, code_tiles, plane_tiles, acc_tiles = {}, {}, {}, {}, {}, {}
+        u_tiles, sum_tiles, dev_tiles, rstd_tiles, offset_tiles = {}, {}, {}, {}, {}
+        v_tiles, back_tiles, x_tiles, y_tiles = {}, {}, {}, {}
 
         def load_h(i):
             h_sb = h_pool.tile([P, TILES, K], BF16)
@@ -108,30 +120,36 @@ def tile_transformerconvblock_pc_t_kernel(
             out=shift[:], in0=ln_b_bf[:], scalar1=scale_norm_col[:, 0:1], scalar2=None, op0=ALU.mult
         )
 
-        def load_x(q):
+        def load_x(first):
             x_sb = x_pool.tile([P, X_GROUP, PAIR, PIXELS], BF16)
             nc.sync.dma_start(
                 out=x_sb[:].rearrange("c b j x -> c b (j x)"),
-                in_=x[q * X_GROUP : (q + 1) * X_GROUP].rearrange("b (c j) y x -> c b (j y x)", j=PAIR),
+                in_=x[first : first + X_GROUP].rearrange("b (c j) y x -> c b (j y x)", j=PAIR),
             )
-            x_tiles[q] = x_sb
+            x_tiles[first // X_GROUP] = x_sb
 
         def transpose_h(i):
-            grouped = mx_pool.tile([P, TILES * PASSES * P * PACK], BF16, align_bytes=64)
-            grouped_words = grouped[:].bitcast(F32).rearrange(
-                "p (t g x w) -> p t g x w", t=TILES, g=PASSES, w=2
-            )
+            words_of_pass = K // PASSES // 2
             for t in range(TILES):
                 h_words = h_tiles[i][:, t, :].bitcast(F32)
                 h_t = psum_h.tile([P, PASSES, 2, P], F32)
                 for g in range(PASSES):
                     for w in range(2):
-                        first = g * (K // PASSES // 2) + w
                         nc.tensor.transpose(
-                            h_t[:, g, w, :], h_words[:, first : (g + 1) * (K // PASSES // 2) : 2], ident[:]
+                            h_t[:, g, w, :],
+                            h_words[:, g * words_of_pass + w : (g + 1) * words_of_pass : 2],
+                            ident[:],
                         )
-                nc.scalar.copy(out=grouped_words[:, t], in_=h_t[:].rearrange("p g w x -> p g x w"))
-            grouped_tiles[i] = grouped
+                h_t_tiles[i, t] = h_t
+
+        def copy_h(i, t):
+            if t == 0:
+                grouped = mx_pool.tile([P, TILES * PASSES * P * PACK], BF16, align_bytes=64)
+                grouped_tiles[i] = grouped
+            grouped_words = grouped_tiles[i][:].bitcast(F32).rearrange(
+                "p (t g x w) -> p t g x w", t=TILES, g=PASSES, w=2
+            )
+            nc.scalar.copy(out=grouped_words[:, t], in_=h_t_tiles[i, t][:].rearrange("p g w x -> p g x w"))
 
         def quantise(i):
             codes = mx_pool.tile([P, TILES * PASSES * P], U32, align_bytes=64)
@@ -171,9 +189,7 @@ def tile_transformerconvblock_pc_t_kernel(
                 )
             u_tiles[i], sum_tiles[i] = u, u_sum
 
-        def statistics(i):
-            neg_mean = stat_pool.tile([P, TILES], F32)
-            nc.scalar.mul(out=neg_mean[:], in_=sum_tiles[i][:], mul=-1.0 / CH)
+        def square_deviations(i):
             dev_sq_sum = stat_pool.tile([P, TILES], F32)
             for t in range(TILES):
                 squares = norm_pool.tile([P, CH], F32)
@@ -181,47 +197,52 @@ def tile_transformerconvblock_pc_t_kernel(
                     out=squares[:],
                     in_=u_tiles[i][:, t].rearrange("p j c -> p (j c)"),
                     func=ACT.Square,
-                    bias=neg_mean[:, t : t + 1],
-                    scale=1.0,
+                    bias=sum_tiles[i][:, t : t + 1],
+                    scale=-float(CH),
                     accum_out=dev_sq_sum[:, t : t + 1],
                 )
+            dev_tiles[i] = dev_sq_sum
+
+        def reciprocal_std(i):
             rstd = stat_pool.tile([P, TILES], F32)
             nc.scalar.activation(
-                out=rstd[:], in_=dev_sq_sum[:], func=ACT.Abs_reciprocal_sqrt, bias=EPS, scale=1.0 / CH
+                out=rstd[:], in_=dev_tiles[i][:], func=ACT.Abs_reciprocal_sqrt, bias=EPS, scale=1.0 / CH**3
             )
-            mean_tiles[i], rstd_tiles[i] = neg_mean, rstd
+            rstd_tiles[i] = rstd
 
-        def normalise_on_scalar(i, v):
-            neg_mean_rstd = stat_pool.tile([P, 1], F32)
-            nc.scalar.activation(
-                out=neg_mean_rstd[:], in_=mean_tiles[i][:, 1:2], func=ACT.Copy, scale=rstd_tiles[i][:, 1:2]
-            )
-            nc.scalar.activation(
-                out=v[:, 1].rearrange("p j c -> p (j c)"),
-                in_=u_tiles[i][:, 1].rearrange("p j c -> p (j c)"),
-                func=ACT.Identity,
-                bias=neg_mean_rstd[:, 0:1],
-                scale=rstd_tiles[i][:, 1:2],
-            )
-
-        def normalise_on_vector(i, v):
-            nc.vector.tensor_scalar(
-                out=v[:, 0],
-                in0=u_tiles[i][:, 0],
-                scalar1=mean_tiles[i][:, 0:1],
-                scalar2=rstd_tiles[i][:, 0:1],
-                op0=ALU.add,
+        def mean_offset(i):
+            offset = stat_pool.tile([P, TILES], F32)
+            nc.vector.scalar_tensor_tensor(
+                out=offset[:],
+                in0=sum_tiles[i][:],
+                scalar=-1.0 / CH,
+                in1=rstd_tiles[i][:],
+                op0=ALU.mult,
                 op1=ALU.mult,
             )
+            offset_tiles[i] = offset
+
+        def normalise(i):
+            v = norm_pool.tile([P, TILES, PAIR, P], F32)
+            for t in range(TILES):
+                nc.vector.tensor_scalar(
+                    out=v[:, t],
+                    in0=u_tiles[i][:, t],
+                    scalar1=rstd_tiles[i][:, t : t + 1],
+                    scalar2=offset_tiles[i][:, t : t + 1],
+                    op0=ALU.mult,
+                    op1=ALU.add,
+                )
+            v_tiles[i] = v
 
         def transpose_back(i):
-            back = psum_out.tile([P, PAIR, TILES, P], F32)
+            back = psum_back.tile([P, PAIR, TILES, P], F32)
             for j in range(PAIR):
                 for t in range(TILES):
                     nc.tensor.transpose(back[:, j, t, :], v_tiles[i][:, t, j, :], ident[:])
             back_tiles[i] = back
 
-        def finish(i):
+        def add_shortcut(i):
             y = y_pool.tile([P, PAIR, PIXELS], F32)
             for j in range(PAIR):
                 nc.vector.scalar_tensor_tensor(
@@ -232,37 +253,38 @@ def tile_transformerconvblock_pc_t_kernel(
                     op0=ALU.mult,
                     op1=ALU.add,
                 )
-            for j in range(PAIR):
-                nc.vector.tensor_scalar(
-                    out=y[:, j, :], in0=y[:, j, :], scalar1=shift[:, j : j + 1], scalar2=0.0, op0=ALU.add, op1=ALU.max
-                )
+            y_tiles[i] = y
+
+        def relu_and_store(i):
+            y = y_tiles[i]
+            nc.vector.tensor_scalar(
+                out=y[:, 0, :], in0=y[:, 0, :], scalar1=shift[:, 0:1], scalar2=0.0, op0=ALU.add, op1=ALU.max
+            )
+            nc.scalar.activation(out=y[:, 1, :], in_=y[:, 1, :], func=ACT.Relu, bias=shift[:, 1:2], scale=1.0)
             nc.sync.dma_start(
                 out=out[i].rearrange("(c j) y x -> c (j y x)", j=PAIR), in_=y[:].rearrange("c j x -> c (j x)")
             )
 
-        def live(i):
-            return 0 <= i < IMAGES
+        def run(stage, i, *more):
+            if 0 <= i < IMAGES:
+                stage(i, *more)
 
-        for s in range(IMAGES + 4):
-            if live(s + H_AHEAD):
-                load_h(s + H_AHEAD)
-            if s % X_GROUP == 0 and live(s):
-                load_x(s // X_GROUP)
-            if live(s - 3):
-                statistics(s - 3)
-                v = norm_pool.tile([P, TILES, PAIR, P], F32)
-                v_tiles[s - 3] = v
-                normalise_on_scalar(s - 3, v)
-            if live(s - 4):
-                transpose_back(s - 4)
-            if live(s):
-                transpose_h(s)
-            if live(s - 1):
-                quantise(s - 1)
-                multiply(s - 1)
-            if live(s - 2):
-                add_bias(s - 2)
-            if live(s - 3):
-                normalise_on_vector(s - 3, v_tiles[s - 3])
-            if live(s - 4):
-                finish(s - 4)
+        for s in range(IMAGES + AT_RELU):
+            run(load_h, s + H_AHEAD)
+            if (s + X_AHEAD - AT_SHORTCUT) % X_GROUP == 0:
+                run(load_x, s + X_AHEAD - AT_SHORTCUT)
+            run(transpose_back, s - AT_BACK)
+            run(transpose_h, s)
+            run(multiply, s - AT_MULTIPLY)
+
+            run(square_deviations, s - AT_STATISTICS)
+            run(copy_h, s - AT_COPY, 0)
+            run(reciprocal_std, s - AT_STATISTICS)
+            run(copy_h, s - AT_COPY, 1)
+
+            run(mean_offset, s - AT_NORMALISE)
+            run(quantise, s - AT_QUANTISE)
+            run(normalise, s - AT_NORMALISE)
+            run(add_bias, s - AT_BIAS)
+            run(add_shortcut, s - AT_SHORTCUT)
+            run(relu_and_store, s - AT_RELU)

@@ -24,7 +24,7 @@ CH = 256
 PAIR = CH // P
 EPS = 1e-5
 X_GROUP = 4
-H_AHEAD = 3
+H_AHEAD = 6
 X_AHEAD = 4
 
 AT_COPY = 1
@@ -261,7 +261,7 @@ def tile_transformerconvblock_pc_t_kernel(
                 out=y[:, 0, :], in0=y[:, 0, :], scalar1=shift[:, 0:1], scalar2=0.0, op0=ALU.add, op1=ALU.max
             )
             nc.scalar.activation(out=y[:, 1, :], in_=y[:, 1, :], func=ACT.Relu, bias=shift[:, 1:2], scale=1.0)
-            nc.sync.dma_start(
+            nc.gpsimd.dma_start(
                 out=out[i].rearrange("(c j) y x -> c (j y x)", j=PAIR), in_=y[:].rearrange("c j x -> c (j x)")
             )
 

@@ -24,7 +24,7 @@ CH = 256
 PAIR = CH // P
 EPS = 1e-5
 X_GROUP = 4
-H_AHEAD = 6
+H_AHEAD = 3
 X_AHEAD = 4
 
 AT_COPY = 1
@@ -60,7 +60,7 @@ def tile_transformerconvblock_pc_t_kernel(
         stack.enter_context(tc.manual_schedule())
 
         h_tiles, h_t_tiles, grouped_tiles, code_tiles, plane_tiles, acc_tiles = {}, {}, {}, {}, {}, {}
-        u_tiles, sum_tiles, dev_tiles, rstd_tiles, offset_tiles = {}, {}, {}, {}, {}
+        u_tiles, sum_tiles, dev_tiles, rstd_tiles, mean_tiles = {}, {}, {}, {}, {}
         v_tiles, back_tiles, x_tiles, y_tiles = {}, {}, {}, {}
 
         def load_h(i):
@@ -210,17 +210,10 @@ def tile_transformerconvblock_pc_t_kernel(
             )
             rstd_tiles[i] = rstd
 
-        def mean_offset(i):
-            offset = stat_pool.tile([P, TILES], F32)
-            nc.vector.scalar_tensor_tensor(
-                out=offset[:],
-                in0=sum_tiles[i][:],
-                scalar=-1.0 / CH,
-                in1=rstd_tiles[i][:],
-                op0=ALU.mult,
-                op1=ALU.mult,
-            )
-            offset_tiles[i] = offset
+        def negative_mean(i):
+            neg_mean = stat_pool.tile([P, TILES], F32)
+            nc.scalar.mul(out=neg_mean[:], in_=sum_tiles[i][:], mul=-1.0 / CH)
+            mean_tiles[i] = neg_mean
 
         def normalise(i):
             v = norm_pool.tile([P, TILES, PAIR, P], F32)
@@ -228,10 +221,10 @@ def tile_transformerconvblock_pc_t_kernel(
                 nc.vector.tensor_scalar(
                     out=v[:, t],
                     in0=u_tiles[i][:, t],
-                    scalar1=rstd_tiles[i][:, t : t + 1],
-                    scalar2=offset_tiles[i][:, t : t + 1],
-                    op0=ALU.mult,
-                    op1=ALU.add,
+                    scalar1=mean_tiles[i][:, t : t + 1],
+                    scalar2=rstd_tiles[i][:, t : t + 1],
+                    op0=ALU.add,
+                    op1=ALU.mult,
                 )
             v_tiles[i] = v
 
@@ -255,13 +248,21 @@ def tile_transformerconvblock_pc_t_kernel(
                 )
             y_tiles[i] = y
 
+        def relu_on_scalar(y, j):
+            nc.scalar.activation(
+                out=y[:, j, :], in_=y[:, j, :], func=ACT.Relu, bias=shift[:, j : j + 1], scale=1.0
+            )
+
         def relu_and_store(i):
             y = y_tiles[i]
-            nc.vector.tensor_scalar(
-                out=y[:, 0, :], in0=y[:, 0, :], scalar1=shift[:, 0:1], scalar2=0.0, op0=ALU.add, op1=ALU.max
-            )
-            nc.scalar.activation(out=y[:, 1, :], in_=y[:, 1, :], func=ACT.Relu, bias=shift[:, 1:2], scale=1.0)
-            nc.gpsimd.dma_start(
+            if i % 2 == 0:
+                nc.vector.tensor_scalar(
+                    out=y[:, 0, :], in0=y[:, 0, :], scalar1=shift[:, 0:1], scalar2=0.0, op0=ALU.add, op1=ALU.max
+                )
+            else:
+                relu_on_scalar(y, 0)
+            relu_on_scalar(y, 1)
+            nc.sync.dma_start(
                 out=out[i].rearrange("(c j) y x -> c (j y x)", j=PAIR), in_=y[:].rearrange("c j x -> c (j x)")
             )
 
@@ -280,9 +281,9 @@ def tile_transformerconvblock_pc_t_kernel(
             run(square_deviations, s - AT_STATISTICS)
             run(copy_h, s - AT_COPY, 0)
             run(reciprocal_std, s - AT_STATISTICS)
+            run(negative_mean, s - AT_STATISTICS)
             run(copy_h, s - AT_COPY, 1)
 
-            run(mean_offset, s - AT_NORMALISE)
             run(quantise, s - AT_QUANTISE)
             run(normalise, s - AT_NORMALISE)
             run(add_bias, s - AT_BIAS)

@@ -33,9 +33,9 @@ AT_MULTIPLY = 3
 AT_BIAS = 4
 AT_STATISTICS = 5
 AT_NORMALISE = 6
-AT_BACK = 7
-AT_SHORTCUT = 8
-AT_RELU = 9
+AT_BACK = 8
+AT_SHORTCUT = 9
+AT_RELU = 10
 
 FLOPS = 2 * IMAGES * PIXELS * K * CH
 
@@ -50,8 +50,8 @@ def tile_transformerconvblock_pc_t_kernel(
         const = stack.enter_context(tc.tile_pool(name="const", bufs=1))
         h_pool = stack.enter_context(tc.tile_pool(name="h_pool", bufs=H_AHEAD + 2))
         mx_pool = stack.enter_context(tc.tile_pool(name="mx_pool", bufs=3))
-        norm_pool = stack.enter_context(tc.tile_pool(name="norm_pool", bufs=4))
-        stat_pool = stack.enter_context(tc.tile_pool(name="stat_pool", bufs=4))
+        norm_pool = stack.enter_context(tc.tile_pool(name="norm_pool", bufs=5))
+        stat_pool = stack.enter_context(tc.tile_pool(name="stat_pool", bufs=5))
         x_pool = stack.enter_context(tc.tile_pool(name="x_pool", bufs=2))
         y_pool = stack.enter_context(tc.tile_pool(name="y_pool", bufs=4))
         psum_h = stack.enter_context(tc.psum_pool(name="psum_h", bufs=2 * TILES))
@@ -218,7 +218,7 @@ def tile_transformerconvblock_pc_t_kernel(
         def normalise(i):
             v = norm_pool.tile([P, TILES, PAIR, P], F32)
             for t in range(TILES):
-                nc.vector.tensor_scalar(
+                nc.gpsimd.tensor_scalar(
                     out=v[:, t],
                     in0=u_tiles[i][:, t],
                     scalar1=mean_tiles[i][:, t : t + 1],
@@ -248,20 +248,12 @@ def tile_transformerconvblock_pc_t_kernel(
                 )
             y_tiles[i] = y
 
-        def relu_on_scalar(y, j):
-            nc.scalar.activation(
-                out=y[:, j, :], in_=y[:, j, :], func=ACT.Relu, bias=shift[:, j : j + 1], scale=1.0
-            )
-
         def relu_and_store(i):
             y = y_tiles[i]
-            if i % 2 == 0:
-                nc.vector.tensor_scalar(
-                    out=y[:, 0, :], in0=y[:, 0, :], scalar1=shift[:, 0:1], scalar2=0.0, op0=ALU.add, op1=ALU.max
-                )
-            else:
-                relu_on_scalar(y, 0)
-            relu_on_scalar(y, 1)
+            nc.vector.tensor_scalar(
+                out=y[:, 0, :], in0=y[:, 0, :], scalar1=shift[:, 0:1], scalar2=0.0, op0=ALU.add, op1=ALU.max
+            )
+            nc.scalar.activation(out=y[:, 1, :], in_=y[:, 1, :], func=ACT.Relu, bias=shift[:, 1:2], scale=1.0)
             nc.sync.dma_start(
                 out=out[i].rearrange("(c j) y x -> c (j y x)", j=PAIR), in_=y[:].rearrange("c j x -> c (j x)")
             )

@@ -212,7 +212,9 @@ def tile_transformerconvblock_pc_t_kernel(
 
         def negative_mean(i):
             neg_mean = stat_pool.tile([P, TILES], F32)
-            nc.scalar.mul(out=neg_mean[:], in_=sum_tiles[i][:], mul=-1.0 / CH)
+            nc.gpsimd.tensor_scalar(
+                out=neg_mean[:], in0=sum_tiles[i][:], scalar1=-1.0 / CH, scalar2=0.0, op0=ALU.mult, op1=ALU.add
+            )
             mean_tiles[i] = neg_mean
 
         def normalise(i):

@@ -23,9 +23,6 @@ PASSES = K // (P * PACK)
 CH = 256
 PAIR = CH // P
 EPS = 1e-5
-X_GROUP = 4
-H_AHEAD = 3
-X_AHEAD = 4
 
 AT_COPY = 1
 AT_QUANTISE = 2
@@ -36,6 +33,16 @@ AT_NORMALISE = 6
 AT_BACK = 8
 AT_SHORTCUT = 9
 AT_RELU = 10
+
+H_AHEAD = 3
+X_GROUP = 4
+X_AHEAD = 4
+
+H_BUFS = H_AHEAD + 2
+MX_BUFS = 3
+NORM_BUFS = AT_BACK - AT_BIAS + 1
+X_BUFS = 2
+Y_BUFS = AT_RELU - AT_SHORTCUT + 3
 
 FLOPS = 2 * IMAGES * PIXELS * K * CH
 
@@ -48,12 +55,12 @@ def tile_transformerconvblock_pc_t_kernel(
 
     with ExitStack() as stack:
         const = stack.enter_context(tc.tile_pool(name="const", bufs=1))
-        h_pool = stack.enter_context(tc.tile_pool(name="h_pool", bufs=H_AHEAD + 2))
-        mx_pool = stack.enter_context(tc.tile_pool(name="mx_pool", bufs=3))
-        norm_pool = stack.enter_context(tc.tile_pool(name="norm_pool", bufs=5))
-        stat_pool = stack.enter_context(tc.tile_pool(name="stat_pool", bufs=5))
-        x_pool = stack.enter_context(tc.tile_pool(name="x_pool", bufs=2))
-        y_pool = stack.enter_context(tc.tile_pool(name="y_pool", bufs=4))
+        h_pool = stack.enter_context(tc.tile_pool(name="h_pool", bufs=H_BUFS))
+        mx_pool = stack.enter_context(tc.tile_pool(name="mx_pool", bufs=MX_BUFS))
+        norm_pool = stack.enter_context(tc.tile_pool(name="norm_pool", bufs=NORM_BUFS))
+        stat_pool = stack.enter_context(tc.tile_pool(name="stat_pool", bufs=NORM_BUFS))
+        x_pool = stack.enter_context(tc.tile_pool(name="x_pool", bufs=X_BUFS))
+        y_pool = stack.enter_context(tc.tile_pool(name="y_pool", bufs=Y_BUFS))
         psum_h = stack.enter_context(tc.psum_pool(name="psum_h", bufs=2 * TILES))
         psum_acc = stack.enter_context(tc.psum_pool(name="psum_acc", bufs=2))
         psum_back = stack.enter_context(tc.psum_pool(name="psum_back", bufs=2))
@@ -96,6 +103,11 @@ def tile_transformerconvblock_pc_t_kernel(
         nc.scalar.dma_start(out=ln_w_bf[:], in_=ln2_w.rearrange("(c j) -> c j", j=PAIR))
         ln_b_bf = const.tile([P, PAIR], BF16)
         nc.scalar.dma_start(out=ln_b_bf[:], in_=ln2_b.rearrange("(c j) -> c j", j=PAIR))
+
+        one = const.tile([P, 1], F32)
+        nc.vector.memset(one[:], 1.0)
+        warm = const.tile([P, 1], F32)
+        nc.scalar.activation(out=warm[:], in_=one[:], func=ACT.Abs_reciprocal_sqrt)
 
         ident = const.tile([P, P], F32)
         make_identity(nc, ident[:])
@@ -212,9 +224,7 @@ def tile_transformerconvblock_pc_t_kernel(
 
         def negative_mean(i):
             neg_mean = stat_pool.tile([P, TILES], F32)
-            nc.gpsimd.tensor_scalar(
-                out=neg_mean[:], in0=sum_tiles[i][:], scalar1=-1.0 / CH, scalar2=0.0, op0=ALU.mult, op1=ALU.add
-            )
+            nc.scalar.mul(out=neg_mean[:], in_=sum_tiles[i][:], mul=-1.0 / CH)
             mean_tiles[i] = neg_mean
 
         def normalise(i):
@@ -268,6 +278,7 @@ def tile_transformerconvblock_pc_t_kernel(
             run(load_h, s + H_AHEAD)
             if (s + X_AHEAD - AT_SHORTCUT) % X_GROUP == 0:
                 run(load_x, s + X_AHEAD - AT_SHORTCUT)
+
             run(transpose_back, s - AT_BACK)
             run(transpose_h, s)
             run(multiply, s - AT_MULTIPLY)

@@ -262,9 +262,12 @@ def tile_transformerconvblock_pc_t_kernel(
 
         def relu_and_store(i):
             y = y_tiles[i]
-            nc.vector.tensor_scalar(
-                out=y[:, 0, :], in0=y[:, 0, :], scalar1=shift[:, 0:1], scalar2=0.0, op0=ALU.add, op1=ALU.max
-            )
+            if i + AT_RELU <= IMAGES - 1 + AT_COPY:
+                nc.vector.tensor_scalar(
+                    out=y[:, 0, :], in0=y[:, 0, :], scalar1=shift[:, 0:1], scalar2=0.0, op0=ALU.add, op1=ALU.max
+                )
+            else:
+                nc.scalar.activation(out=y[:, 0, :], in_=y[:, 0, :], func=ACT.Relu, bias=shift[:, 0:1], scale=1.0)
             nc.scalar.activation(out=y[:, 1, :], in_=y[:, 1, :], func=ACT.Relu, bias=shift[:, 1:2], scale=1.0)
             nc.sync.dma_start(
                 out=out[i].rearrange("(c j) y x -> c (j y x)", j=PAIR), in_=y[:].rearrange("c j x -> c (j x)")

@@ -26,13 +26,13 @@ EPS = 1e-5
 
 AT_COPY = 1
 AT_QUANTISE = 2
-AT_MULTIPLY = 3
-AT_BIAS = 4
-AT_STATISTICS = 5
-AT_NORMALISE = 6
-AT_BACK = 8
-AT_SHORTCUT = 9
-AT_RELU = 10
+AT_MULTIPLY = 2
+AT_BIAS = 3
+AT_STATISTICS = 4
+AT_NORMALISE = 4
+AT_BACK = 6
+AT_SHORTCUT = 6
+AT_RELU = 7
 
 H_AHEAD = 3
 X_GROUP = 4
@@ -284,6 +284,7 @@ def tile_transformerconvblock_pc_t_kernel(
 
             run(transpose_back, s - AT_BACK)
             run(transpose_h, s)
+            run(quantise, s - AT_QUANTISE)
             run(multiply, s - AT_MULTIPLY)
 
             run(square_deviations, s - AT_STATISTICS)
@@ -292,7 +293,6 @@ def tile_transformerconvblock_pc_t_kernel(
             run(negative_mean, s - AT_STATISTICS)
             run(copy_h, s - AT_COPY, 1)
 
-            run(quantise, s - AT_QUANTISE)
             run(normalise, s - AT_NORMALISE)
             run(add_bias, s - AT_BIAS)
             run(add_shortcut, s - AT_SHORTCUT)

@@ -23,6 +23,9 @@ PASSES = K // (P * PACK)
 CH = 256
 PAIR = CH // P
 EPS = 1e-5
+AT_SCALE_FFN = CH
+AT_SCALE_NORM = CH + 16
+ROW = CH + 32
 
 AT_COPY = 1
 AT_QUANTISE = 2
@@ -42,7 +45,7 @@ H_BUFS = H_AHEAD + 2
 MX_BUFS = 3
 NORM_BUFS = AT_BACK - AT_BIAS + 1
 X_BUFS = 2
-Y_BUFS = AT_RELU - AT_SHORTCUT + 3
+Y_BUFS = AT_RELU - AT_SHORTCUT + 5
 
 FLOPS = 2 * IMAGES * PIXELS * K * CH
 
@@ -79,6 +82,7 @@ def tile_transformerconvblock_pc_t_kernel(
             h_tiles[i] = h_sb
 
         load_h(0)
+        load_h(1)
         w_words = const.tile([P, PASSES, 2 * CH], U8, align_bytes=64)
         nc.sync.dma_start(
             out=w_words[:].bitcast(I32), in_=ffn2_w_words.bitcast(I32).rearrange("g p n -> p g n")
@@ -90,15 +94,18 @@ def tile_transformerconvblock_pc_t_kernel(
                 out=w_planes[32 * quad : 32 * quad + 4].bitcast(I32),
                 in_=ffn2_w_scales[:, 4 * quad : 4 * quad + 4, :].bitcast(I32).rearrange("g r n -> r g n"),
             )
-        for i in range(1, H_AHEAD):
+        for i in range(2, H_AHEAD):
             load_h(i)
 
-        bias_bf = const.tile([P, CH], BF16)
-        nc.scalar.dma_start(out=bias_bf[:], in_=ffn2_b.partition_broadcast(P))
-        scale_ffn_bf = const.tile([P, 1], BF16)
-        nc.scalar.dma_start(out=scale_ffn_bf[:], in_=scale_ffn.partition_broadcast(P))
-        scale_norm_bf = const.tile([P, 1], BF16)
-        nc.scalar.dma_start(out=scale_norm_bf[:], in_=scale_norm2.partition_broadcast(P))
+        row = const.tile([P, ROW], BF16)
+        nc.vector.memset(row[:], 0.0)
+        nc.scalar.dma_start(out=row[0:1, 0:CH], in_=ffn2_b.rearrange("(o c) -> o c", o=1))
+        nc.scalar.dma_start(out=row[0:1, AT_SCALE_FFN : AT_SCALE_FFN + 1], in_=scale_ffn.rearrange("(o c) -> o c", o=1))
+        nc.scalar.dma_start(
+            out=row[0:1, AT_SCALE_NORM : AT_SCALE_NORM + 1], in_=scale_norm2.rearrange("(o c) -> o c", o=1)
+        )
+        ones = const.tile([P, P], BF16)
+        nc.vector.memset(ones[:], 1.0)
         ln_w_bf = const.tile([P, PAIR], BF16)
         nc.scalar.dma_start(out=ln_w_bf[:], in_=ln2_w.rearrange("(c j) -> c j", j=PAIR))
         ln_b_bf = const.tile([P, PAIR], BF16)
@@ -111,26 +118,31 @@ def tile_transformerconvblock_pc_t_kernel(
 
         ident = const.tile([P, P], F32)
         make_identity(nc, ident[:])
+
         scale_ffn_col = const.tile([P, 1], F32)
-        nc.vector.tensor_copy(out=scale_ffn_col[:], in_=scale_ffn_bf[:])
         bias_scaled = const.tile([P, PAIR, P], F32)
-        nc.vector.tensor_scalar(
-            out=bias_scaled[:],
-            in0=bias_bf[:].rearrange("p (c j) -> p j c", j=PAIR),
-            scalar1=scale_ffn_col[:, 0:1],
-            scalar2=None,
-            op0=ALU.mult,
-        )
-        scale_norm_col = const.tile([P, 1], F32)
-        nc.vector.tensor_copy(out=scale_norm_col[:], in_=scale_norm_bf[:])
         gain = const.tile([P, PAIR], F32)
-        nc.vector.tensor_scalar(
-            out=gain[:], in0=ln_w_bf[:], scalar1=scale_norm_col[:, 0:1], scalar2=None, op0=ALU.mult
-        )
         shift = const.tile([P, PAIR], F32)
-        nc.vector.tensor_scalar(
-            out=shift[:], in0=ln_b_bf[:], scalar1=scale_norm_col[:, 0:1], scalar2=None, op0=ALU.mult
-        )
+
+        def spread_constants():
+            back = psum_back.tile([P, ROW], F32)
+            nc.tensor.matmul(back[:], lhsT=ones[:], rhs=row[:], start=True, stop=True)
+            nc.vector.tensor_copy(out=scale_ffn_col[:], in_=back[:, AT_SCALE_FFN : AT_SCALE_FFN + 1])
+            nc.vector.tensor_scalar(
+                out=bias_scaled[:],
+                in0=back[:, 0:CH].rearrange("p (c j) -> p j c", j=PAIR),
+                scalar1=scale_ffn_col[:, 0:1],
+                scalar2=None,
+                op0=ALU.mult,
+            )
+            scale_norm_col = const.tile([P, 1], F32)
+            nc.vector.tensor_copy(out=scale_norm_col[:], in_=back[:, AT_SCALE_NORM : AT_SCALE_NORM + 1])
+            nc.vector.tensor_scalar(
+                out=gain[:], in0=ln_w_bf[:], scalar1=scale_norm_col[:, 0:1], scalar2=None, op0=ALU.mult
+            )
+            nc.vector.tensor_scalar(
+                out=shift[:], in0=ln_b_bf[:], scalar1=scale_norm_col[:, 0:1], scalar2=None, op0=ALU.mult
+            )
 
         def load_x(first):
             x_sb = x_pool.tile([P, X_GROUP, PAIR, PIXELS], BF16)
@@ -284,6 +296,8 @@ def tile_transformerconvblock_pc_t_kernel(
 
             run(transpose_back, s - AT_BACK)
             run(transpose_h, s)
+            if s == 0:
+                spread_constants()
             run(quantise, s - AT_QUANTISE)
             run(multiply, s - AT_MULTIPLY)
 

@@ -25,7 +25,10 @@ PAIR = CH // P
 EPS = 1e-5
 AT_SCALE_FFN = CH
 AT_SCALE_NORM = CH + 16
-ROW = CH + 32
+SPREAD = CH + 32
+AT_LN_W = SPREAD
+AT_LN_B = SPREAD + CH
+ROW = SPREAD + 2 * CH
 
 AT_COPY = 1
 AT_QUANTISE = 2
@@ -81,8 +84,8 @@ def tile_transformerconvblock_pc_t_kernel(
             )
             h_tiles[i] = h_sb
 
-        load_h(0)
-        load_h(1)
+        for i in range(H_AHEAD):
+            load_h(i)
         w_words = const.tile([P, PASSES, 2 * CH], U8, align_bytes=64)
         nc.sync.dma_start(
             out=w_words[:].bitcast(I32), in_=ffn2_w_words.bitcast(I32).rearrange("g p n -> p g n")
@@ -94,8 +97,6 @@ def tile_transformerconvblock_pc_t_kernel(
                 out=w_planes[32 * quad : 32 * quad + 4].bitcast(I32),
                 in_=ffn2_w_scales[:, 4 * quad : 4 * quad + 4, :].bitcast(I32).rearrange("g r n -> r g n"),
             )
-        for i in range(2, H_AHEAD):
-            load_h(i)
 
         row = const.tile([P, ROW], BF16)
         nc.vector.memset(row[:], 0.0)
@@ -106,10 +107,8 @@ def tile_transformerconvblock_pc_t_kernel(
         )
         ones = const.tile([P, P], BF16)
         nc.vector.memset(ones[:], 1.0)
-        ln_w_bf = const.tile([P, PAIR], BF16)
-        nc.scalar.dma_start(out=ln_w_bf[:], in_=ln2_w.rearrange("(c j) -> c j", j=PAIR))
-        ln_b_bf = const.tile([P, PAIR], BF16)
-        nc.scalar.dma_start(out=ln_b_bf[:], in_=ln2_b.rearrange("(c j) -> c j", j=PAIR))
+        nc.scalar.dma_start(out=row[0:1, AT_LN_W : AT_LN_W + CH], in_=ln2_w.rearrange("(o c) -> o c", o=1))
+        nc.scalar.dma_start(out=row[0:1, AT_LN_B : AT_LN_B + CH], in_=ln2_b.rearrange("(o c) -> o c", o=1))
 
         one = const.tile([P, 1], F32)
         nc.vector.memset(one[:], 1.0)
@@ -125,8 +124,16 @@ def tile_transformerconvblock_pc_t_kernel(
         shift = const.tile([P, PAIR], F32)
 
         def spread_constants():
-            back = psum_back.tile([P, ROW], F32)
-            nc.tensor.matmul(back[:], lhsT=ones[:], rhs=row[:], start=True, stop=True)
+            back = psum_back.tile([P, SPREAD + 2 * PAIR], F32)
+            nc.tensor.matmul(back[:, 0:SPREAD], lhsT=ones[:], rhs=row[:, 0:SPREAD], start=True, stop=True)
+            for n, first in enumerate((AT_LN_W, AT_LN_W + 1, AT_LN_B, AT_LN_B + 1)):
+                nc.tensor.matmul(
+                    back[:, SPREAD + n : SPREAD + n + 1],
+                    lhsT=row[:, first : first + CH - 1 : PAIR],
+                    rhs=ones[:, 0:1],
+                    start=True,
+                    stop=True,
+                )
             nc.vector.tensor_copy(out=scale_ffn_col[:], in_=back[:, AT_SCALE_FFN : AT_SCALE_FFN + 1])
             nc.vector.tensor_scalar(
                 out=bias_scaled[:],
@@ -138,10 +145,10 @@ def tile_transformerconvblock_pc_t_kernel(
             scale_norm_col = const.tile([P, 1], F32)
             nc.vector.tensor_copy(out=scale_norm_col[:], in_=back[:, AT_SCALE_NORM : AT_SCALE_NORM + 1])
             nc.vector.tensor_scalar(
-                out=gain[:], in0=ln_w_bf[:], scalar1=scale_norm_col[:, 0:1], scalar2=None, op0=ALU.mult
+                out=gain[:], in0=back[:, SPREAD : SPREAD + PAIR], scalar1=scale_norm_col[:, 0:1], scalar2=None, op0=ALU.mult
             )
             nc.vector.tensor_scalar(
-                out=shift[:], in0=ln_b_bf[:], scalar1=scale_norm_col[:, 0:1], scalar2=None, op0=ALU.mult
+                out=shift[:], in0=back[:, SPREAD + PAIR : SPREAD + 2 * PAIR], scalar1=scale_norm_col[:, 0:1], scalar2=None, op0=ALU.mult
             )
 
         def load_x(first):
@@ -240,9 +247,10 @@ def tile_transformerconvblock_pc_t_kernel(
             mean_tiles[i] = neg_mean
 
         def normalise(i):
+            engine = nc.gpsimd if i + AT_NORMALISE <= IMAGES - 1 + AT_BIAS else nc.vector
             v = norm_pool.tile([P, TILES, PAIR, P], F32)
             for t in range(TILES):
-                nc.gpsimd.tensor_scalar(
+                engine.tensor_scalar(
                     out=v[:, t],
                     in0=u_tiles[i][:, t],
                     scalar1=mean_tiles[i][:, t : t + 1],
@@ -307,7 +315,7 @@ def tile_transformerconvblock_pc_t_kernel(
             run(negative_mean, s - AT_STATISTICS)
             run(copy_h, s - AT_COPY, 1)
 
-            run(normalise, s - AT_NORMALISE)
             run(add_bias, s - AT_BIAS)
             run(add_shortcut, s - AT_SHORTCUT)
+            run(normalise, s - AT_NORMALISE)
             run(relu_and_store, s - AT_RELU)

@@ -84,6 +84,18 @@ def tile_transformerconvblock_pc_t_kernel(
             )
             h_tiles[i] = h_sb
 
+        row = const.tile([P, ROW], BF16)
+        nc.vector.memset(row[:], 0.0)
+        nc.scalar.dma_start(out=row[0:1, 0:CH], in_=ffn2_b.rearrange("(o c) -> o c", o=1))
+        nc.scalar.dma_start(out=row[0:1, AT_SCALE_FFN : AT_SCALE_FFN + 1], in_=scale_ffn.rearrange("(o c) -> o c", o=1))
+        nc.scalar.dma_start(
+            out=row[0:1, AT_SCALE_NORM : AT_SCALE_NORM + 1], in_=scale_norm2.rearrange("(o c) -> o c", o=1)
+        )
+        ones = const.tile([P, P], BF16)
+        nc.vector.memset(ones[:], 1.0)
+        nc.scalar.dma_start(out=row[0:1, AT_LN_W : AT_LN_W + CH], in_=ln2_w.rearrange("(o c) -> o c", o=1))
+        nc.scalar.dma_start(out=row[0:1, AT_LN_B : AT_LN_B + CH], in_=ln2_b.rearrange("(o c) -> o c", o=1))
+
         for i in range(H_AHEAD):
             load_h(i)
         w_words = const.tile([P, PASSES, 2 * CH], U8, align_bytes=64)
@@ -97,18 +109,6 @@ def tile_transformerconvblock_pc_t_kernel(
                 out=w_planes[32 * quad : 32 * quad + 4].bitcast(I32),
                 in_=ffn2_w_scales[:, 4 * quad : 4 * quad + 4, :].bitcast(I32).rearrange("g r n -> r g n"),
             )
-
-        row = const.tile([P, ROW], BF16)
-        nc.vector.memset(row[:], 0.0)
-        nc.scalar.dma_start(out=row[0:1, 0:CH], in_=ffn2_b.rearrange("(o c) -> o c", o=1))
-        nc.scalar.dma_start(out=row[0:1, AT_SCALE_FFN : AT_SCALE_FFN + 1], in_=scale_ffn.rearrange("(o c) -> o c", o=1))
-        nc.scalar.dma_start(
-            out=row[0:1, AT_SCALE_NORM : AT_SCALE_NORM + 1], in_=scale_norm2.rearrange("(o c) -> o c", o=1)
-        )
-        ones = const.tile([P, P], BF16)
-        nc.vector.memset(ones[:], 1.0)
-        nc.scalar.dma_start(out=row[0:1, AT_LN_W : AT_LN_W + CH], in_=ln2_w.rearrange("(o c) -> o c", o=1))
-        nc.scalar.dma_start(out=row[0:1, AT_LN_B : AT_LN_B + CH], in_=ln2_b.rearrange("(o c) -> o c", o=1))
 
         one = const.tile([P, 1], F32)
         nc.vector.memset(one[:], 1.0)
@@ -304,9 +304,9 @@ def tile_transformerconvblock_pc_t_kernel(
 
             run(transpose_back, s - AT_BACK)
             run(transpose_h, s)
-            if s == 0:
-                spread_constants()
             run(quantise, s - AT_QUANTISE)
+            if s == AT_BIAS - 1:
+                spread_constants()
             run(multiply, s - AT_MULTIPLY)
 
             run(square_deviations, s - AT_STATISTICS)

@@ -23,6 +23,7 @@ PASSES = K // (P * PACK)
 CH = 256
 PAIR = CH // P
 EPS = 1e-5
+WARM_UP = 4
 AT_SCALE_FFN = CH
 AT_SCALE_NORM = CH + 16
 SPREAD = CH + 32
@@ -84,6 +85,19 @@ def tile_transformerconvblock_pc_t_kernel(
             )
             h_tiles[i] = h_sb
 
+        one = const.tile([P, 1], F32)
+        nc.vector.memset(one[:], 1.0)
+        warm = const.tile([P, 1], F32)
+        nc.scalar.activation(out=warm[:], in_=one[:], func=ACT.Abs_reciprocal_sqrt)
+
+        ones = const.tile([P, P], BF16)
+        nc.vector.memset(ones[:], 1.0)
+        zeros = const.tile([P, TILES * CH], BF16)
+        nc.vector.memset(zeros[:], 0.0)
+        acc = psum_acc.tile([P, TILES, CH], F32)
+        for n in range(WARM_UP):
+            nc.tensor.matmul(acc[:].rearrange("p t c -> p (t c)"), lhsT=ones[:], rhs=zeros[:], start=True, stop=True)
+
         row = const.tile([P, ROW], BF16)
         nc.vector.memset(row[:], 0.0)
         nc.scalar.dma_start(out=row[0:1, 0:CH], in_=ffn2_b.rearrange("(o c) -> o c", o=1))
@@ -91,8 +105,6 @@ def tile_transformerconvblock_pc_t_kernel(
         nc.scalar.dma_start(
             out=row[0:1, AT_SCALE_NORM : AT_SCALE_NORM + 1], in_=scale_norm2.rearrange("(o c) -> o c", o=1)
         )
-        ones = const.tile([P, P], BF16)
-        nc.vector.memset(ones[:], 1.0)
         nc.scalar.dma_start(out=row[0:1, AT_LN_W : AT_LN_W + CH], in_=ln2_w.rearrange("(o c) -> o c", o=1))
         nc.scalar.dma_start(out=row[0:1, AT_LN_B : AT_LN_B + CH], in_=ln2_b.rearrange("(o c) -> o c", o=1))
 
@@ -109,11 +121,6 @@ def tile_transformerconvblock_pc_t_kernel(
                 out=w_planes[32 * quad : 32 * quad + 4].bitcast(I32),
                 in_=ffn2_w_scales[:, 4 * quad : 4 * quad + 4, :].bitcast(I32).rearrange("g r n -> r g n"),
             )
-
-        one = const.tile([P, 1], F32)
-        nc.vector.memset(one[:], 1.0)
-        warm = const.tile([P, 1], F32)
-        nc.scalar.activation(out=warm[:], in_=one[:], func=ACT.Abs_reciprocal_sqrt)
 
         ident = const.tile([P, P], F32)
         make_identity(nc, ident[:])

@@ -110,11 +110,11 @@ def tile_transformerconvblock_pc_t_kernel(
 
         for i in range(H_AHEAD):
             load_h(i)
-        w_words = const.tile([P, PASSES, 2 * CH], U8, align_bytes=64)
+        w_words = const.tile([P, PASSES, 2 * CH], U8, align_bytes=256)
         nc.sync.dma_start(
             out=w_words[:].bitcast(I32), in_=ffn2_w_words.bitcast(I32).rearrange("g p n -> p g n")
         )
-        w_planes = const.tile([P, PASSES, CH], U8, align_bytes=64)
+        w_planes = const.tile([P, PASSES, CH], U8, align_bytes=256)
         nc.vector.memset(w_planes[:].bitcast(I32), 0)
         for quad in range(4):
             nc.sync.dma_start(
@@ -182,7 +182,7 @@ def tile_transformerconvblock_pc_t_kernel(
 
         def copy_h(i, t):
             if t == 0:
-                grouped = mx_pool.tile([P, TILES * PASSES * P * PACK], BF16, align_bytes=64)
+                grouped = mx_pool.tile([P, TILES * PASSES * P * PACK], BF16, align_bytes=256)
                 grouped_tiles[i] = grouped
             grouped_words = grouped_tiles[i][:].bitcast(F32).rearrange(
                 "p (t g x w) -> p t g x w", t=TILES, g=PASSES, w=2
@@ -190,8 +190,8 @@ def tile_transformerconvblock_pc_t_kernel(
             nc.scalar.copy(out=grouped_words[:, t], in_=h_t_tiles[i, t][:].rearrange("p g w x -> p g x w"))
 
         def quantise(i):
-            codes = mx_pool.tile([P, TILES * PASSES * P], U32, align_bytes=64)
-            planes = mx_pool.tile([P, TILES * PASSES * P], U8, align_bytes=64)
+            codes = mx_pool.tile([P, TILES * PASSES * P], U32, align_bytes=256)
+            planes = mx_pool.tile([P, TILES * PASSES * P], U8, align_bytes=256)
             nc.vector.quantize_mx(out=codes[:].bitcast(FP8X4), scales=planes[:], in_=grouped_tiles[i][:])
             code_tiles[i], plane_tiles[i] = codes, planes
 
@@ -199,7 +199,8 @@ def tile_transformerconvblock_pc_t_kernel(
             acc = psum_acc.tile([P, TILES, CH], F32)
             for t in range(TILES):
                 for n in range(CH // P):
-                    for g in range(PASSES):
+                    order = range(PASSES) if n == 0 else range(PASSES - 1, -1, -1)
+                    for g in order:
                         pixels = slice((t * PASSES + g) * P, (t * PASSES + g + 1) * P)
                         nc.tensor.matmul_mx(
                             out=acc[:, t, n * P : (n + 1) * P],
@@ -207,8 +208,8 @@ def tile_transformerconvblock_pc_t_kernel(
                             lhsT_scale=plane_tiles[i][:, pixels],
                             rhs=w_words[:, g, 2 * n * P : 2 * (n + 1) * P].bitcast(FP4X4),
                             rhs_scale=w_planes[:, g, n * P : (n + 1) * P],
-                            start=(g == 0),
-                            stop=(g == PASSES - 1),
+                            start=(g == order[0]),
+                            stop=(g == order[-1]),
                         )
             acc_tiles[i] = acc
 

from contextlib import ExitStack

import concourse.mybir as mybir
from concourse.masks import make_identity

F32 = mybir.dt.float32
BF16 = mybir.dt.bfloat16
I32 = mybir.dt.int32
U32 = mybir.dt.uint32
U8 = mybir.dt.uint8
FP8X4 = mybir.dt.float8_e4m3fn_x4
FP4X4 = mybir.dt.float4_e2m1fn_x4
ACT = mybir.ActivationFunctionType
ALU = mybir.AluOpType

P = 128
PACK = 4
IMAGES = 32
PIXELS = 256
TILES = PIXELS // P
K = 1024
PASSES = K // (P * PACK)
CH = 256
PAIR = CH // P
EPS = 1e-5
WARM_UP = 4
AT_SCALE_FFN = CH
AT_SCALE_NORM = CH + 16
SPREAD = CH + 32
AT_LN_W = SPREAD
AT_LN_B = SPREAD + CH
ROW = SPREAD + 2 * CH

AT_COPY = 1
AT_QUANTISE = 2
AT_MULTIPLY = 2
AT_BIAS = 3
AT_STATISTICS = 4
AT_NORMALISE = 4
AT_BACK = 6
AT_SHORTCUT = 6
AT_RELU = 7

H_AHEAD = 3
X_GROUP = 4
X_AHEAD = 4

H_BUFS = H_AHEAD + 2
MX_BUFS = 3
NORM_BUFS = AT_BACK - AT_BIAS + 1
X_BUFS = 2
Y_BUFS = AT_RELU - AT_SHORTCUT + 5

FLOPS = 2 * IMAGES * PIXELS * K * CH


def tile_transformerconvblock_pc_t_kernel(
    tc, h, ffn2_w_words, ffn2_w_scales, ffn2_b, scale_ffn, ln2_w, ln2_b, scale_norm2, x, out
):
    nc = tc.nc
    h_rows = h.flatten_outer_dims()

    with ExitStack() as stack:
        const = stack.enter_context(tc.tile_pool(name="const", bufs=1))
        h_pool = stack.enter_context(tc.tile_pool(name="h_pool", bufs=H_BUFS))
        mx_pool = stack.enter_context(tc.tile_pool(name="mx_pool", bufs=MX_BUFS))
        norm_pool = stack.enter_context(tc.tile_pool(name="norm_pool", bufs=NORM_BUFS))
        stat_pool = stack.enter_context(tc.tile_pool(name="stat_pool", bufs=NORM_BUFS))
        x_pool = stack.enter_context(tc.tile_pool(name="x_pool", bufs=X_BUFS))
        y_pool = stack.enter_context(tc.tile_pool(name="y_pool", bufs=Y_BUFS))
        psum_h = stack.enter_context(tc.psum_pool(name="psum_h", bufs=2 * TILES))
        psum_acc = stack.enter_context(tc.psum_pool(name="psum_acc", bufs=2))
        psum_back = stack.enter_context(tc.psum_pool(name="psum_back", bufs=2))
        stack.enter_context(tc.manual_schedule())

        h_tiles, h_t_tiles, grouped_tiles, code_tiles, plane_tiles, acc_tiles = {}, {}, {}, {}, {}, {}
        u_tiles, sum_tiles, dev_tiles, rstd_tiles, mean_tiles = {}, {}, {}, {}, {}
        v_tiles, back_tiles, x_tiles, y_tiles = {}, {}, {}, {}

        def load_h(i):
            h_sb = h_pool.tile([P, TILES, K], BF16)
            nc.sync.dma_start(
                out=h_sb[:],
                in_=h_rows[i * PIXELS : (i + 1) * PIXELS, :].rearrange("(p t) k -> p t k", t=TILES),
            )
            h_tiles[i] = h_sb

        one = const.tile([P, 1], F32)
        nc.vector.memset(one[:], 1.0)
        warm = const.tile([P, 1], F32)
        nc.scalar.activation(out=warm[:], in_=one[:], func=ACT.Abs_reciprocal_sqrt)

        ones = const.tile([P, P], BF16)
        nc.vector.memset(ones[:], 1.0)
        zeros = const.tile([P, TILES * CH], BF16)
        nc.vector.memset(zeros[:], 0.0)
        acc = psum_acc.tile([P, TILES, CH], F32)
        for n in range(WARM_UP):
            nc.tensor.matmul(acc[:].rearrange("p t c -> p (t c)"), lhsT=ones[:], rhs=zeros[:], start=True, stop=True)

        row = const.tile([P, ROW], BF16)
        nc.vector.memset(row[:], 0.0)
        nc.scalar.dma_start(out=row[0:1, 0:CH], in_=ffn2_b.rearrange("(o c) -> o c", o=1))
        nc.scalar.dma_start(out=row[0:1, AT_SCALE_FFN : AT_SCALE_FFN + 1], in_=scale_ffn.rearrange("(o c) -> o c", o=1))
        nc.scalar.dma_start(
            out=row[0:1, AT_SCALE_NORM : AT_SCALE_NORM + 1], in_=scale_norm2.rearrange("(o c) -> o c", o=1)
        )
        nc.scalar.dma_start(out=row[0:1, AT_LN_W : AT_LN_W + CH], in_=ln2_w.rearrange("(o c) -> o c", o=1))
        nc.scalar.dma_start(out=row[0:1, AT_LN_B : AT_LN_B + CH], in_=ln2_b.rearrange("(o c) -> o c", o=1))

        for i in range(H_AHEAD):
            load_h(i)
        w_words = const.tile([P, PASSES, 2 * CH], U8, align_bytes=256)
        nc.sync.dma_start(
            out=w_words[:].bitcast(I32), in_=ffn2_w_words.bitcast(I32).rearrange("g p n -> p g n")
        )
        w_planes = const.tile([P, PASSES, CH], U8, align_bytes=256)
        nc.vector.memset(w_planes[:].bitcast(I32), 0)
        for quad in range(4):
            nc.sync.dma_start(
                out=w_planes[32 * quad : 32 * quad + 4].bitcast(I32),
                in_=ffn2_w_scales[:, 4 * quad : 4 * quad + 4, :].bitcast(I32).rearrange("g r n -> r g n"),
            )

        ident = const.tile([P, P], F32)
        make_identity(nc, ident[:])

        scale_ffn_col = const.tile([P, 1], F32)
        bias_scaled = const.tile([P, PAIR, P], F32)
        gain = const.tile([P, PAIR], F32)
        shift = const.tile([P, PAIR], F32)

        def spread_constants():
            back = psum_back.tile([P, SPREAD + 2 * PAIR], F32)
            nc.tensor.matmul(back[:, 0:SPREAD], lhsT=ones[:], rhs=row[:, 0:SPREAD], start=True, stop=True)
            for n, first in enumerate((AT_LN_W, AT_LN_W + 1, AT_LN_B, AT_LN_B + 1)):
                nc.tensor.matmul(
                    back[:, SPREAD + n : SPREAD + n + 1],
                    lhsT=row[:, first : first + CH - 1 : PAIR],
                    rhs=ones[:, 0:1],
                    start=True,
                    stop=True,
                )
            nc.vector.tensor_copy(out=scale_ffn_col[:], in_=back[:, AT_SCALE_FFN : AT_SCALE_FFN + 1])
            nc.vector.tensor_scalar(
                out=bias_scaled[:],
                in0=back[:, 0:CH].rearrange("p (c j) -> p j c", j=PAIR),
                scalar1=scale_ffn_col[:, 0:1],
                scalar2=None,
                op0=ALU.mult,
            )
            scale_norm_col = const.tile([P, 1], F32)
            nc.vector.tensor_copy(out=scale_norm_col[:], in_=back[:, AT_SCALE_NORM : AT_SCALE_NORM + 1])
            nc.vector.tensor_scalar(
                out=gain[:], in0=back[:, SPREAD : SPREAD + PAIR], scalar1=scale_norm_col[:, 0:1], scalar2=None, op0=ALU.mult
            )
            nc.vector.tensor_scalar(
                out=shift[:], in0=back[:, SPREAD + PAIR : SPREAD + 2 * PAIR], scalar1=scale_norm_col[:, 0:1], scalar2=None, op0=ALU.mult
            )

        def load_x(first):
            x_sb = x_pool.tile([P, X_GROUP, PAIR, PIXELS], BF16)
            nc.sync.dma_start(
                out=x_sb[:].rearrange("c b j x -> c b (j x)"),
                in_=x[first : first + X_GROUP].rearrange("b (c j) y x -> c b (j y x)", j=PAIR),
            )
            x_tiles[first // X_GROUP] = x_sb

        def transpose_h(i):
            words_of_pass = K // PASSES // 2
            for t in range(TILES):
                h_words = h_tiles[i][:, t, :].bitcast(F32)
                h_t = psum_h.tile([P, PASSES, 2, P], F32)
                for g in range(PASSES):
                    for w in range(2):
                        nc.tensor.transpose(
                            h_t[:, g, w, :],
                            h_words[:, g * words_of_pass + w : (g + 1) * words_of_pass : 2],
                            ident[:],
                        )
                h_t_tiles[i, t] = h_t

        def copy_h(i, t):
            if t == 0:
                grouped = mx_pool.tile([P, TILES * PASSES * P * PACK], BF16, align_bytes=256)
                grouped_tiles[i] = grouped
            grouped_words = grouped_tiles[i][:].bitcast(F32).rearrange(
                "p (t g x w) -> p t g x w", t=TILES, g=PASSES, w=2
            )
            nc.scalar.copy(out=grouped_words[:, t], in_=h_t_tiles[i, t][:].rearrange("p g w x -> p g x w"))

        def quantise(i):
            codes = mx_pool.tile([P, TILES * PASSES * P], U32, align_bytes=256)
            planes = mx_pool.tile([P, TILES * PASSES * P], U8, align_bytes=256)
            nc.vector.quantize_mx(out=codes[:].bitcast(FP8X4), scales=planes[:], in_=grouped_tiles[i][:])
            code_tiles[i], plane_tiles[i] = codes, planes

        def multiply(i):
            acc = psum_acc.tile([P, TILES, CH], F32)
            for t in range(TILES):
                for n in range(CH // P):
                    order = range(PASSES) if n == 0 else range(PASSES - 1, -1, -1)
                    for g in order:
                        pixels = slice((t * PASSES + g) * P, (t * PASSES + g + 1) * P)
                        nc.tensor.matmul_mx(
                            out=acc[:, t, n * P : (n + 1) * P],
                            lhsT=code_tiles[i][:, pixels].bitcast(FP8X4),
                            lhsT_scale=plane_tiles[i][:, pixels],
                            rhs=w_words[:, g, 2 * n * P : 2 * (n + 1) * P].bitcast(FP4X4),
                            rhs_scale=w_planes[:, g, n * P : (n + 1) * P],
                            start=(g == order[0]),
                            stop=(g == order[-1]),
                        )
            acc_tiles[i] = acc

        def add_bias(i):
            u = norm_pool.tile([P, TILES, PAIR, P], F32)
            u_sum = stat_pool.tile([P, TILES], F32)
            for t in range(TILES):
                nc.vector.scalar_tensor_tensor(
                    out=u[:, t],
                    in0=acc_tiles[i][:, t, :].rearrange("p (c j) -> p j c", j=PAIR),
                    scalar=scale_ffn_col[:, 0:1],
                    in1=bias_scaled[:],
                    op0=ALU.mult,
                    op1=ALU.add,
                    accum_out=u_sum[:, t : t + 1],
                )
            u_tiles[i], sum_tiles[i] = u, u_sum

        def square_deviations(i):
            dev_sq_sum = stat_pool.tile([P, TILES], F32)
            for t in range(TILES):
                squares = norm_pool.tile([P, CH], F32)
                nc.scalar.activation(
                    out=squares[:],
                    in_=u_tiles[i][:, t].rearrange("p j c -> p (j c)"),
                    func=ACT.Square,
                    bias=sum_tiles[i][:, t : t + 1],
                    scale=-float(CH),
                    accum_out=dev_sq_sum[:, t : t + 1],
                )
            dev_tiles[i] = dev_sq_sum

        def reciprocal_std(i):
            rstd = stat_pool.tile([P, TILES], F32)
            nc.scalar.activation(
                out=rstd[:], in_=dev_tiles[i][:], func=ACT.Abs_reciprocal_sqrt, bias=EPS, scale=1.0 / CH**3
            )
            rstd_tiles[i] = rstd

        def negative_mean(i):
            neg_mean = stat_pool.tile([P, TILES], F32)
            nc.scalar.mul(out=neg_mean[:], in_=sum_tiles[i][:], mul=-1.0 / CH)
            mean_tiles[i] = neg_mean

        def normalise(i):
            engine = nc.gpsimd if i + AT_NORMALISE <= IMAGES - 1 + AT_BIAS else nc.vector
            v = norm_pool.tile([P, TILES, PAIR, P], F32)
            for t in range(TILES):
                engine.tensor_scalar(
                    out=v[:, t],
                    in0=u_tiles[i][:, t],
                    scalar1=mean_tiles[i][:, t : t + 1],
                    scalar2=rstd_tiles[i][:, t : t + 1],
                    op0=ALU.add,
                    op1=ALU.mult,
                )
            v_tiles[i] = v

        def transpose_back(i):
            back = psum_back.tile([P, PAIR, TILES, P], F32)
            for j in range(PAIR):
                for t in range(TILES):
                    nc.tensor.transpose(back[:, j, t, :], v_tiles[i][:, t, j, :], ident[:])
            back_tiles[i] = back

        def add_shortcut(i):
            y = y_pool.tile([P, PAIR, PIXELS], F32)
            for j in range(PAIR):
                nc.vector.scalar_tensor_tensor(
                    out=y[:, j, :].rearrange("c (p t) -> c p t", t=TILES),
                    in0=back_tiles[i][:, j].rearrange("c t p -> c p t"),
                    scalar=gain[:, j : j + 1],
                    in1=x_tiles[i // X_GROUP][:, i % X_GROUP, j, :].rearrange("c (p t) -> c p t", t=TILES),
                    op0=ALU.mult,
                    op1=ALU.add,
                )
            y_tiles[i] = y

        def relu_and_store(i):
            y = y_tiles[i]
            if i + AT_RELU <= IMAGES - 1 + AT_COPY:
                nc.vector.tensor_scalar(
                    out=y[:, 0, :], in0=y[:, 0, :], scalar1=shift[:, 0:1], scalar2=0.0, op0=ALU.add, op1=ALU.max
                )
            else:
                nc.scalar.activation(out=y[:, 0, :], in_=y[:, 0, :], func=ACT.Relu, bias=shift[:, 0:1], scale=1.0)
            nc.scalar.activation(out=y[:, 1, :], in_=y[:, 1, :], func=ACT.Relu, bias=shift[:, 1:2], scale=1.0)
            nc.sync.dma_start(
                out=out[i].rearrange("(c j) y x -> c (j y x)", j=PAIR), in_=y[:].rearrange("c j x -> c (j x)")
            )

        def run(stage, i, *more):
            if 0 <= i < IMAGES:
                stage(i, *more)

        for s in range(IMAGES + AT_RELU):
            run(load_h, s + H_AHEAD)
            if (s + X_AHEAD - AT_SHORTCUT) % X_GROUP == 0:
                run(load_x, s + X_AHEAD - AT_SHORTCUT)

            run(transpose_back, s - AT_BACK)
            run(transpose_h, s)
            run(quantise, s - AT_QUANTISE)
            if s == AT_BIAS - 1:
                spread_constants()
            run(multiply, s - AT_MULTIPLY)

            run(square_deviations, s - AT_STATISTICS)
            run(copy_h, s - AT_COPY, 0)
            run(reciprocal_std, s - AT_STATISTICS)
            run(negative_mean, s - AT_STATISTICS)
            run(copy_h, s - AT_COPY, 1)

            run(add_bias, s - AT_BIAS)
            run(add_shortcut, s - AT_SHORTCUT)
            run(normalise, s - AT_NORMALISE)
            run(relu_and_store, s - AT_RELU)
